import numpy as np
import ml_dtypes


def mxq(x, axis, fmt="e4m3"):
    dtype, down = {"e4m3": (ml_dtypes.float8_e4m3fn, 7), "e5m2": (ml_dtypes.float8_e5m2, 14)}[fmt]
    v = np.moveaxis(np.asarray(x, np.float32).astype(ml_dtypes.bfloat16).astype(np.float64), axis, -1)
    blocks = v.reshape(v.shape[:-1] + (-1, 32))
    amax = np.abs(blocks).max(-1, keepdims=True)
    byte = np.maximum(np.where(amax > 0, np.frexp(amax)[1] - 1 + 127, 0) - down, 1)
    scale = np.exp2(byte - 127.0)
    codes = (blocks / scale).astype(np.float32).astype(dtype).astype(np.float64)
    return np.moveaxis((codes * scale).reshape(v.shape), -1, axis)


WIDE = False


def mx_kscale(k):
    if not WIDE:
        return np.ones(k)
    levels = np.array([10, -10, 5, -5, 0])
    if k % 512:
        return np.exp2(np.random.permutation(np.resize(levels, k // 32))).repeat(32)
    a = np.empty((k // 512, 16))
    for p in range(k // 512):
        a[p, :8] = np.random.permutation(np.resize(levels, 8))
        for g in range(8):
            far = levels[np.abs(levels - a[p, g]) >= 10]
            a[p, g + 8] = far[np.random.randint(len(far))]
    return np.exp2(a.ravel()).repeat(32)


BF16 = ml_dtypes.bfloat16


def bf(x):
    return np.asarray(x, np.float32).astype(BF16)


def f64(x):
    return np.asarray(x).astype(np.float64)


B, N, D = 8, 1024, 128
C = B * 2 * D


def sigmoid(u):
    return 1.0 / (1.0 + np.exp(-u))


def flat(a):
    return a.transpose(1, 0, 2).reshape(N, C)


def setup_inputs():
    s = mx_kscale(C).reshape(B, 2, D)[:, 0, :][:, None, :]
    u = mx_kscale(N)
    q = bf(np.random.standard_normal((B, N, D)))
    k0 = bf(np.random.standard_normal((B, N, D)))
    v = bf(np.random.standard_normal((B, N, D)) * 0.125 * np.sqrt(N))
    bias0 = bf(np.random.standard_normal((N, N)))
    g = bf(np.random.standard_normal((B, N, D)) * np.exp2(np.random.randint(-6, 1, (B, N, 1))) * 32.0 * u[None, :, None] / s)
    eb0 = np.exp(f64(bias0))
    ek0 = np.exp(f64(k0))
    den = eb0 @ ek0
    num = eb0 @ (ek0 * f64(v))
    lse = np.log(den)
    y = num / den
    return {"q": q,
            "k": bf(f64(k0) + np.log(s)),
            "v": v,
            "bias": bf(f64(bias0) - np.log(u)[:, None]),
            "lse": np.asarray(lse, np.float32),
            "y": np.asarray(y, np.float32),
            "grad_out": g}


def reference(q, k, v, bias, lse, y, grad_out):
    vf = f64(v)
    eb = np.exp(f64(bias))
    ek = np.exp(f64(k))
    dn = f64(grad_out) * sigmoid(f64(q)) * np.exp(-f64(lse))
    dd = -dn * f64(y)
    dz = flat(np.concatenate([dn, dd], axis=2))
    xx = flat(np.concatenate([ek * vf, ek], axis=2))
    dxx = mxq(eb, 0, "e4m3").T @ mxq(dz, 0, "e5m2")
    deb = mxq(dz, 1, "e5m2") @ mxq(xx, 1, "e4m3").T
    dxx = dxx.reshape(N, B, 2, D).transpose(1, 0, 2, 3)
    dk = ek * (vf * dxx[:, :, 0, :] + dxx[:, :, 1, :])
    dbias = eb * deb
    return dk, dbias

from contextlib import ExitStack
import math

import concourse.mybir as mybir
from concourse.masks import make_identity

F32 = mybir.dt.float32
BF16 = mybir.dt.bfloat16
U32 = mybir.dt.uint32
U8 = mybir.dt.uint8
E4M3 = mybir.dt.float8_e4m3fn_x4
E5M2 = mybir.dt.float8_e5m2_x4
ACT = mybir.ActivationFunctionType
ALU = mybir.AluOpType

P = 128
B, N, D = 8, 1024, 128
FLOPS = 2 * 2 * N * N * (2 * B * D)
LN2 = math.log(2.0)


def tile_modelnew_v_kernel(tc, q, k, v, bias, lse, y, grad_out, out_0, out_1):
    nc = tc.nc
    tok = "b (g p j) d -> g p b (j d)"
    qv = q.rearrange(tok, p=P, j=4)
    kv = k.rearrange(tok, p=P, j=4)
    vv = v.rearrange(tok, p=P, j=4)
    lv = lse.rearrange(tok, p=P, j=4)
    yv = y.rearrange(tok, p=P, j=4)
    gv = grad_out.rearrange(tok, p=P, j=4)
    biasv = bias.rearrange("(g p j) w -> g p j w", p=P, j=4)
    out0v = out_0.rearrange("b (g p j) d -> g p b j d", p=P, j=4)
    out1v = out_1.rearrange("(g p j) w -> g p j w", p=P, j=4)

    with ExitStack() as ctx:
        keep = ctx.enter_context(tc.tile_pool(name="keep", bufs=1))
        pin = ctx.enter_context(tc.tile_pool(name="pin", bufs=3))
        work = ctx.enter_context(tc.tile_pool(name="work", bufs=2))
        psum = ctx.enter_context(tc.psum_pool(name="psum", bufs=4))

        ident = keep.tile([P, P], F32, name="ident")
        warm = keep.tile([P, 1], F32, name="warm")
        bias_sb = [keep.tile([P, 4, N], BF16, name="bias%d" % g) for g in range(2)]
        ebc = keep.tile([P, 2, N], U32, name="ebc", align_bytes=64)
        ebs = keep.tile([P, 2, N], U8, name="ebs", align_bytes=64)

        inp = {}
        ths = {}
        dns = {}
        dds = {}
        grp = {}
        codes = {}
        eks = {}
        ks = {}
        vs = {}
        ekvs = {}
        tts = {}
        dks = {}
        ebfs = {}
        dbo = {}
        units = [(0, 0), (0, 1), (1, 0), (1, 1)]

        def load_step(s):
            Q, g = units[s // 2]
            b0 = 4 * Q + 2 * (s % 2)
            qt = pin.tile([P, 2, 512], BF16, name="qt", tag="qt")
            lt = pin.tile([P, 2, 512], F32, name="lt", tag="lt")
            gt = pin.tile([P, 2, 512], BF16, name="gt", tag="gt")
            yt = pin.tile([P, 2, 512], F32, name="yt", tag="yt")
            nc.sync.dma_start(out=qt[:], in_=qv[g][:, b0 : b0 + 2, :])
            nc.sync.dma_start(out=gt[:], in_=gv[g][:, b0 : b0 + 2, :])
            nc.sync.dma_start(out=lt[:], in_=lv[g][:, b0 : b0 + 2, :])
            nc.sync.dma_start(out=yt[:], in_=yv[g][:, b0 : b0 + 2, :])
            inp[s] = (qt, lt, gt, yt)

        def load_bias(g):
            nc.sync.dma_start(out=bias_sb[g][:], in_=biasv[g])

        def load_kv(Q, g):
            kt = work.tile([P, 4, 512], BF16, name="kt", tag="kt", bufs=1)
            vt = work.tile([P, 4, 512], BF16, name="vt", tag="vt", bufs=2)
            nc.sync.dma_start(out=kt[:], in_=kv[g][:, 4 * Q : 4 * Q + 4, :])
            nc.sync.dma_start(out=vt[:], in_=vv[g][:, 4 * Q : 4 * Q + 4, :])
            ks[(Q, g)] = kt
            vs[(Q, g)] = vt

        def s_te(s):
            qt, lt, gt, yt = inp[s]
            th = work.tile([P, 2, 512], F32, name="th", tag="th", bufs=2)
            nc.scalar.activation(out=th[:], in_=qt[:], func=ACT.Tanh, scale=0.5)
            nc.scalar.activation(out=lt[:], in_=lt[:], func=ACT.Exp, scale=-1.0, bias=-LN2)
            ths[s] = th

        def v_a(s):
            nc.vector.scalar_tensor_tensor(
                out=ths[s][:], in0=ths[s][:], scalar=1.0, in1=inp[s][2][:], op0=ALU.add, op1=ALU.mult
            )

        def perm(t):
            return t[:].rearrange("p b (j d) -> p j b d", j=4)

        def v_dn(s):
            u, h = s // 2, s % 2
            if h == 0:
                dns[u] = work.tile([P, 4, 4, D], F32, name="dn", tag="dn", bufs=2)
                dds[u] = work.tile([P, 4, 4, D], BF16, name="dd", tag="dd", bufs=3)
            nc.vector.tensor_tensor(
                out=dns[u][:, :, 2 * h : 2 * h + 2, :], in0=perm(ths[s]), in1=perm(inp[s][1]), op=ALU.mult
            )

        def v_dd(s):
            u, h = s // 2, s % 2
            nc.vector.tensor_tensor(
                out=dds[u][:, :, 2 * h : 2 * h + 2, :],
                in0=dns[u][:, :, 2 * h : 2 * h + 2, :],
                in1=perm(inp[s][3]),
                op=ALU.mult,
            )

        def new_grp(key):
            grp[key] = work.tile([P, 512, 4], BF16, name="grp", tag="grp", bufs=5, align_bytes=64)

        def g_copy(s, which, eng):
            u, h = s // 2, s % 2
            if h == 0:
                new_grp(("i", u, which))
            src = (dns if which == 0 else dds)[u]
            o = grp[("i", u, which)][:, 256 * h : 256 * (h + 1), :]
            i = src[:, :, 2 * h : 2 * h + 2, :].rearrange("p j b d -> p (b d) j")
            if eng == "v":
                nc.vector.tensor_copy(out=o, in_=i)
            else:
                nc.scalar.copy(out=o, in_=i)

        def quant(key, ckey, which, dt, tag, bufs):
            if ckey not in codes:
                c = work.tile([P, 1024], U32, name=tag + "c", tag=tag + "c", bufs=bufs, align_bytes=64)
                sc = work.tile([P, 1024], U8, name=tag + "s", tag=tag + "s", bufs=bufs, align_bytes=64)
                codes[ckey] = (c, sc)
            c, sc = codes[ckey]
            w = slice(512 * which, 512 * which + 512)
            nc.vector.quantize_mx(
                out=c[:, w].bitcast(dt), scales=sc[:, w], in_=grp[key][:].rearrange("p c t -> p (c t)")
            )

        def q_i(u, which):
            quant(("i", u, which), ("i", u), which, E5M2, "dzi", 3)

        def q_t(u, which):
            quant(("t", u, which), ("t", u), which, E5M2, "dzt", 4)

        def q_x(Q, g, which):
            quant(("x", Q, g, which), ("x", Q, g), which, E4M3, "xxt", 4)

        pst = {}

        def pe_f32(key, src, j):
            ps = psum.tile([P, 4, P], F32, name="trf", tag="tr", bufs=3)
            flat = src[:, j, :, :].rearrange("p b d -> p (b d)")
            for t in range(4):
                nc.tensor.transpose(ps[:, t, :], flat[:, t::4], ident[:])
            pst[(key, j)] = ps

        def pe_words(key, src, jp):
            ps = psum.tile([P, 2, 2, P], F32, name="trw", tag="tr", bufs=3)
            for jj in range(2):
                flat = src[:, 2 * jp + jj, :, :].rearrange("p b d -> p (b d)").bitcast(F32)
                for w in range(2):
                    nc.tensor.transpose(ps[:, jj, w, :], flat[:, w::2], ident[:])
            pst[(key, jp)] = ps

        def out_f32(key, j, neg):
            if j == 0:
                new_grp(key)
            o = grp[key][:, P * j : P * (j + 1), :]
            i = pst[(key, j)][:].rearrange("m t p -> m p t")
            if neg:
                nc.scalar.activation(out=o, in_=i, func=ACT.Copy, scale=-1.0)
            else:
                nc.scalar.copy(out=o, in_=i)

        def out_words(key, jp):
            if jp == 0:
                new_grp(key)
            o = grp[key][:, 256 * jp : 256 * (jp + 1), :].rearrange("m c t -> m (c t)").bitcast(F32)
            o = o.rearrange("m (j p w) -> m j p w", j=2, w=2)
            nc.scalar.copy(out=o, in_=pst[(key, jp)][:].rearrange("m j w p -> m j p w"))

        def trans(kf, srcf, kw, srcw, neg):
            for j in range(4):
                pe_f32(kf, srcf, j)
                out_f32(kf, j, neg)
            for j in range(2):
                pe_words(kw, srcw, j)
                out_words(kw, j)

        def trans_dz(u):
            trans(("t", u, 0), dns[u], ("t", u, 1), dds[u], False)

        def trans_x(Q, g):
            trans(("x", Q, g, 1), eks[(Q, g)], ("x", Q, g, 0), ekvs[(Q, g)], True)

        def s_eb(g, gj):
            new_grp(("b", g, gj))
            i = bias_sb[g][:, :, 512 * gj : 512 * gj + 512].rearrange("p t (m j) -> p j m t", j=4)
            nc.scalar.activation(
                out=grp[("b", g, gj)][:].rearrange("p (j m) t -> p j m t", j=4), in_=i, func=ACT.Exp
            )

        def q_eb(g, gj):
            w = slice(512 * gj, 512 * gj + 512)
            nc.vector.quantize_mx(
                out=ebc[:, g, w].bitcast(E4M3),
                scales=ebs[:, g, w],
                in_=grp[("b", g, gj)][:].rearrange("p c t -> p (c t)"),
            )

        def s_ek(Q, g):
            t = work.tile([P, 4, 4, D], F32, name="ek", tag="ek", bufs=2)
            kk = perm(ks[(Q, g)])
            for h in range(2):
                nc.scalar.activation(
                    out=t[:, 2 * h : 2 * h + 2, :, :], in_=kk[:, 2 * h : 2 * h + 2, :, :], func=ACT.Exp
                )
            eks[(Q, g)] = t

        def v_ekv(Q, g):
            t = work.tile([P, 4, 4, D], BF16, name="ekv", tag="dd", bufs=3)
            vp = perm(vs[(Q, g)])
            for h in range(2):
                nc.vector.tensor_tensor(
                    out=t[:, 2 * h : 2 * h + 2, :, :],
                    in0=eks[(Q, g)][:, 2 * h : 2 * h + 2, :, :],
                    in1=vp[:, 2 * h : 2 * h + 2, :, :],
                    op=ALU.mult,
                )
            ekvs[(Q, g)] = t

        mmp = {}

        def pe_dxx(Q, gj, jj):
            col = slice(512 * gj + P * jj, 512 * gj + P * (jj + 1))
            for h in range(2):
                ps = psum.tile([P, 512], F32, name="mm", tag="mm", bufs=5)
                for g in range(2):
                    c, sc = codes[("i", 2 * Q + g)]
                    w = slice(512 * h, 512 * h + 512)
                    nc.tensor.matmul_mx(
                        out=ps[:],
                        lhsT=ebc[:, g, col].bitcast(E4M3),
                        lhsT_scale=ebs[:, g, col],
                        rhs=c[:, w].bitcast(E5M2),
                        rhs_scale=sc[:, w],
                        start=(g == 0),
                        stop=(g == 1),
                    )
                mmp[(Q, gj, jj, h)] = ps

        def v_dk(Q, gj, jj, h):
            ps = mmp[(Q, gj, jj, h)][:].rearrange("p (b d) -> p b d", b=4)
            if h == 0:
                t = work.tile([P, 4, D], F32, name="tt", tag="tt", bufs=3)
                tts[(Q, gj, jj)] = t
                vj = vs[(Q, gj)][:, :, P * jj : P * (jj + 1)]
                nc.vector.tensor_tensor(out=t[:], in0=ps, in1=vj, op=ALU.mult)
            else:
                t = tts[(Q, gj, jj)]
                nc.vector.tensor_tensor(out=t[:], in0=t[:], in1=ps, op=ALU.subtract)

        def g_dk(Q, gj, jj, eng):
            if jj % 2 == 0:
                dks[(Q, gj, jj // 2)] = work.tile([P, 4, 2, D], F32, name="dk", tag="dk", bufs=3)
            o = dks[(Q, gj, jj // 2)]
            eng.tensor_tensor(
                out=o[:, :, jj % 2, :], in0=tts[(Q, gj, jj)][:], in1=eks[(Q, gj)][:, jj, :, :], op=ALU.mult
            )
            if jj % 2 == 1:
                nc.sync.dma_start(
                    out=out0v[gj][:, 4 * Q : 4 * Q + 4, jj - 1 : jj + 1, :], in_=o[:]
                )

        def s_ebf(g, jj, gj):
            t = work.tile([P, 512], F32, name="ebf", tag="ebf", bufs=2)
            nc.scalar.activation(out=t[:], in_=bias_sb[g][:, jj, 512 * gj : 512 * gj + 512], func=ACT.Exp)
            ebfs[(g, jj, gj)] = t

        def pe_deb(g, jj, gj):
            ps = psum.tile([P, 512], F32, name="mm", tag="mm", bufs=5)
            col = slice(P * jj, P * (jj + 1))
            for i in range(4):
                Q, h = i // 2, i % 2
                c, sc = codes[("t", 2 * Q + g)]
                xc, xs = codes[("x", Q, gj)]
                lcol = slice(512 * h + P * jj, 512 * h + P * (jj + 1))
                w = slice(512 * h, 512 * h + 512)
                nc.tensor.matmul_mx(
                    out=ps[:],
                    lhsT=c[:, lcol].bitcast(E5M2),
                    lhsT_scale=sc[:, lcol],
                    rhs=xc[:, w].bitcast(E4M3),
                    rhs_scale=xs[:, w],
                    start=(i == 0),
                    stop=(i == 3),
                )
            mmp[("d", g, jj, gj)] = ps

        def v_db(g, jj, gj):
            if gj == 0:
                dbo[(g, jj)] = work.tile([P, N], F32, name="dbo", tag="dbo", bufs=2)
            o = dbo[(g, jj)]
            w = slice(512 * gj, 512 * gj + 512)
            nc.vector.tensor_tensor(
                out=o[:, w].rearrange("p (m j) -> p m j", j=4),
                in0=mmp[("d", g, jj, gj)][:].rearrange("p (j m) -> p m j", j=4),
                in1=ebfs[(g, jj, gj)][:].rearrange("p (m j) -> p m j", j=4),
                op=ALU.mult,
            )
            if gj == 1:
                nc.sync.dma_start(out=out1v[g][:, jj, :], in_=o[:])

        load_step(0)
        load_step(1)
        load_bias(0)
        nc.vector.memset(warm[:], 0.0)
        nc.scalar.activation(out=warm[:], in_=warm[:], func=ACT.Exp)
        make_identity(nc, ident[:])
        with tc.high_priority(offset=0):
            load_step(2)
            load_bias(1)
            s_te(0)
            s_te(1)
            v_a(0)
            v_dn(0)
            v_a(1)
            v_dd(0)
            g_copy(0, 0, "v")
            s_eb(0, 0)
            g_copy(0, 1, "v")
            load_step(3)
            load_kv(0, 0)
            s_te(2)
            v_dn(1)
            v_a(2)
            v_dd(1)
            g_copy(1, 0, "v")
            q_eb(0, 0)
            g_copy(1, 1, "v")
            s_eb(0, 1)
            load_step(4)
            s_te(3)
            v_dn(2)
            q_i(0, 0)
            v_a(3)
            q_i(0, 1)
            v_dd(2)
            q_eb(0, 1)
            trans_dz(0)
            g_copy(2, 0, "v")
            g_copy(2, 1, "v")
            s_eb(1, 0)
            load_kv(0, 1)
            v_dn(3)
            q_t(0, 0)
            s_te(4)
            v_dd(3)
            q_t(0, 1)
            s_eb(1, 1)
            g_copy(3, 0, "v")
            q_eb(1, 0)
            g_copy(3, 1, "v")
            q_eb(1, 1)
            load_step(5)
            s_ek(0, 0)
            v_a(4)
            q_i(1, 0)
            q_i(1, 1)
            for jj in range(4):
                pe_dxx(0, 0, jj)
            trans_dz(1)
            v_ekv(0, 0)
            s_ek(0, 1)
            for jj in range(4):
                v_dk(0, 0, jj, 0)
                v_dk(0, 0, jj, 1)
                g_dk(0, 0, jj, nc.gpsimd)
            trans_x(0, 0)
            s_te(5)
            q_t(1, 0)
            v_ekv(0, 1)
            q_t(1, 1)
            for jj in range(4):
                pe_dxx(0, 1, jj)
            v_dn(4)
            q_x(0, 0, 1)
            for jj in range(4):
                v_dk(0, 1, jj, 0)
                v_dk(0, 1, jj, 1)
                g_dk(0, 1, jj, nc.gpsimd)
            trans_x(0, 1)
            load_step(6)
            load_kv(1, 0)
            load_step(7)
            load_kv(1, 1)
            q_x(0, 0, 0)
            v_a(5)
            v_dd(4)
            s_te(6)
            g_copy(4, 0, "v")
            q_x(0, 1, 1)
            g_copy(4, 1, "v")
            q_x(0, 1, 0)
            v_dn(5)
            v_a(6)
            s_ek(1, 0)
            v_dd(5)
            g_copy(5, 0, "v")
            v_ekv(1, 0)
            g_copy(5, 1, "v")
            trans_dz(2)
            trans_x(1, 0)
            q_i(2, 0)
            s_te(7)
            s_ek(1, 1)
            v_dn(6)
            q_i(2, 1)
            v_a(7)
            v_dd(6)
            v_ekv(1, 1)
            q_t(2, 0)
            g_copy(6, 0, "v")
            q_t(2, 1)
            g_copy(6, 1, "v")
            q_x(1, 0, 1)
            q_x(1, 0, 0)
            trans_x(1, 1)
            v_dn(7)
            s_ebf(0, 0, 0)
            s_ebf(0, 0, 1)
            q_x(1, 1, 1)
            v_dd(7)
            q_x(1, 1, 0)
            g_copy(7, 0, "v")
            for jj in range(4):
                pe_deb(0, jj, 0)
                pe_deb(0, jj, 1)
                if jj == 0:
                    trans_dz(3)
            g_copy(7, 1, "v")
            v_db(0, 0, 0)
            v_db(0, 0, 1)
            q_i(3, 0)
            q_i(3, 1)
            for jj in range(1, 4):
                for gj in range(2):
                    s_ebf(0, jj, gj)
                    v_db(0, jj, gj)
                if jj == 1:
                    q_t(3, 0)
                    q_t(3, 1)
            for gj in range(2):
                for jj in range(4):
                    pe_dxx(1, gj, jj)
                    v_dk(1, gj, jj, 0)
                    v_dk(1, gj, jj, 1)
                    g_dk(1, gj, jj, nc.gpsimd)
            for jj in range(4):
                for gj in range(2):
                    pe_deb(1, jj, gj)
                    s_ebf(1, jj, gj)
                    v_db(1, jj, gj)
